import numpy as np
import ml_dtypes


def mxq(x, axis, fmt="e4m3"):
    dtype, down = {"e4m3": (ml_dtypes.float8_e4m3fn, 7), "e5m2": (ml_dtypes.float8_e5m2, 14)}[fmt]
    v = np.moveaxis(np.asarray(x, np.float32).astype(ml_dtypes.bfloat16).astype(np.float64), axis, -1)
    blocks = v.reshape(v.shape[:-1] + (-1, 32))
    amax = np.abs(blocks).max(-1, keepdims=True)
    byte = np.maximum(np.where(amax > 0, np.frexp(amax)[1] - 1 + 127, 0) - down, 1)
    scale = np.exp2(byte - 127.0)
    codes = (blocks / scale).astype(np.float32).astype(dtype).astype(np.float64)
    return np.moveaxis((codes * scale).reshape(v.shape), -1, axis)


WIDE = False


def mx_kscale(k):
    if not WIDE:
        return np.ones(k)
    levels = np.array([10, -10, 5, -5, 0])
    if k % 512:
        return np.exp2(np.random.permutation(np.resize(levels, k // 32))).repeat(32)
    a = np.empty((k // 512, 16))
    for p in range(k // 512):
        a[p, :8] = np.random.permutation(np.resize(levels, 8))
        for g in range(8):
            far = levels[np.abs(levels - a[p, g]) >= 10]
            a[p, g + 8] = far[np.random.randint(len(far))]
    return np.exp2(a.ravel()).repeat(32)


BF16 = ml_dtypes.bfloat16


def bf(x):
    return np.asarray(x, np.float32).astype(BF16)


def f64(x):
    return np.asarray(x).astype(np.float64)


E2M1 = np.array([0.0, 0.5, 1.0, 1.5, 2.0, 3.0, 4.0, 6.0, -0.0, -0.5, -1.0, -1.5, -2.0, -3.0, -4.0, -6.0])


def pack_weight(w, fmt):
    k, n = w.shape
    w = f64(bf(w)).reshape(k // 32, 32, n)
    amax = np.abs(w).max(1)
    if fmt == "e4m3":
        byte = np.frexp(amax)[1] - 1 + 127 - 7
    else:
        mant, ex = np.frexp(amax / 6.0)
        byte = np.where(mant > 0.5, ex, ex - 1) + 127
    byte = np.clip(np.where(amax > 0, byte, 1), 1, 254)
    scaled = (w * np.exp2(127.0 - byte)[:, None, :]).reshape(k, n).astype(np.float32)
    by_word = np.ascontiguousarray(scaled.reshape(k // 512, 128, 4, n).transpose(0, 1, 3, 2))
    if fmt == "e4m3":
        words = by_word.astype(ml_dtypes.float8_e4m3fn).view(np.uint8)
    else:
        c = by_word.astype(ml_dtypes.float4_e2m1fn).view(np.uint8) & 0xF
        words = c[..., 0::2] | (c[..., 1::2] << 4)
    return np.ascontiguousarray(words), np.ascontiguousarray(byte.astype(np.uint8).reshape(k // 512, 16, n))


def unpack_weight(words, scales, fmt):
    g, p, n, _ = words.shape
    if fmt == "e4m3":
        vals = np.ascontiguousarray(words).view(ml_dtypes.float8_e4m3fn).astype(np.float64)
    else:
        nib = np.empty((g, p, n, 4), np.uint8)
        nib[..., 0::2] = words & 0xF
        nib[..., 1::2] = words >> 4
        vals = E2M1[nib]
    vals = vals * np.repeat(np.exp2(scales.astype(np.float64) - 127.0), 8, axis=1)[..., None]
    return vals.transpose(0, 1, 3, 2).reshape(g * 512, n)


B, S, D, H, QL, KVL, RD, ND, VD = 2, 2048, 1024, 4, 512, 512, 64, 64, 128
QHD = ND + RD
ROPE_THETA, ROPE_RATIO = 10000.0, 1.0


def rope_tables(seq_len):
    half = RD // 2
    inv_freq = ROPE_RATIO / (ROPE_THETA ** (np.arange(half) * 2.0 / RD))
    freqs = np.arange(seq_len)[:, None] * inv_freq[None, :]
    return np.cos(freqs), np.sin(freqs)


def apply_rope(x, cos, sin):
    x_even = x[..., 0::2]
    x_odd = x[..., 1::2]
    r_even = x_even * cos - x_odd * sin
    r_odd = x_odd * cos + x_even * sin
    return np.stack([r_even, r_odd], axis=-1).reshape(x.shape)


def draw0():
    s, t = mx_kscale(D), mx_kscale(QL)
    hidden_states = bf(np.random.standard_normal((B, S, D)) * s)
    Wqa_words, Wqa_scales = pack_weight(np.random.standard_normal((D, QL)) / np.sqrt(D) / s[:, None] * t, "e4m3")
    Wqb_words, Wqb_scales = pack_weight(np.random.standard_normal((QL, H * QHD)) / np.sqrt(QL) / t[:, None], "e4m3")
    return {"hidden_states": hidden_states,
            "Wqa_words": Wqa_words, "Wqa_scales": Wqa_scales,
            "Wqb_words": Wqb_words, "Wqb_scales": Wqb_scales}


def core(hidden_states, Wqa_words, Wqa_scales, Wqb_words, Wqb_scales):
    q_latent = mxq(f64(hidden_states), 2, "e4m3") @ unpack_weight(Wqa_words, Wqa_scales, "e4m3")
    q = (mxq(q_latent, 2, "e4m3") @ unpack_weight(Wqb_words, Wqb_scales, "e4m3")).reshape(B, S, H, QHD)
    q = q.transpose(0, 2, 1, 3)
    q_nope, q_pe = q[..., :ND], q[..., ND:]
    cos, sin = rope_tables(S)
    q_pe = apply_rope(q_pe, cos, sin)
    return np.concatenate([q_nope, q_pe], axis=-1)


def e4m3fn_bytes(y):
    return np.clip(np.asarray(y, np.float64), -448.0, 448.0).astype(np.float32).astype(ml_dtypes.float8_e4m3fn).view(np.uint8)


def e4m3fn_values(b):
    return np.asarray(b, np.uint8).view(ml_dtypes.float8_e4m3fn).astype(np.float64)


def setup_inputs():
    d = draw0()
    x0 = np.asarray(d['hidden_states']).astype(np.float64)
    s = (np.max(np.abs(x0), axis=(0, 1), keepdims=True) / 448.0).astype(np.float32)
    out = {}
    for k, v in d.items():
        if k == 'hidden_states':
            out['hidden_states_bytes'] = e4m3fn_bytes(x0 / s.astype(np.float64))
            out['hidden_states_scale'] = s
        else:
            out[k] = v
    return out


def reference(hidden_states_bytes, hidden_states_scale, Wqa_words, Wqa_scales, Wqb_words, Wqb_scales):
    return core(e4m3fn_values(hidden_states_bytes) * hidden_states_scale.astype(np.float64), Wqa_words, Wqa_scales, Wqb_words, Wqb_scales)

@@ -1,0 +1,305 @@
+import math
+from contextlib import ExitStack
+
+import concourse.mybir as mybir
+from concourse.masks import make_identity
+
+B, S, D, QL = 2, 2048, 1024, 512
+H, ND, RD = 4, 64, 64
+HD = ND + RD
+P = 128
+GROUPS = 8
+J = 2
+TILES = B * J
+TOK = TILES * P
+HALF = RD // 2
+FLOPS = 2 * B * S * QL * (D + H * HD)
+
+F32 = mybir.dt.float32
+BF16 = mybir.dt.bfloat16
+I32 = mybir.dt.int32
+U8 = mybir.dt.uint8
+FP8 = mybir.dt.float8_e4m3fn
+FP8X4 = mybir.dt.float8_e4m3fn_x4
+MULT = mybir.AluOpType.mult
+ADD = mybir.AluOpType.add
+SUB = mybir.AluOpType.subtract
+AF = mybir.ActivationFunctionType
+
+
+def tile_mlaattention_pa_t_w8_kernel(
+    tc, x_bytes, x_scale, wqa_words, wqa_scales, wqb_words, wqb_scales, out
+):
+    nc = tc.nc
+    with ExitStack() as ctx:
+        keep = ctx.enter_context(tc.tile_pool(name="keep", bufs=1))
+        xin = ctx.enter_context(tc.tile_pool(name="xin", bufs=3))
+        work = ctx.enter_context(tc.tile_pool(name="work", bufs=2))
+        prod = ctx.enter_context(tc.tile_pool(name="prod", bufs=4))
+        outs = ctx.enter_context(tc.tile_pool(name="outs", bufs=4))
+        ps_t = ctx.enter_context(tc.psum_pool(name="ps_t", bufs=2))
+        ps_l = ctx.enter_context(tc.psum_pool(name="ps_l", bufs=2))
+        ps_n = ctx.enter_context(tc.psum_pool(name="ps_n", bufs=2))
+        ps_p = ctx.enter_context(tc.psum_pool(name="ps_p", bufs=2))
+
+        x_view = x_bytes.rearrange("b (g p j) k -> g p b (j k)", p=P, j=J)
+        out_view = out.rearrange("b h (g p j) d -> g p (b h) (j d)", p=P, j=J)
+
+        ident = keep.tile([P, P], F32, name="ident")
+        scale = keep.tile([P, D], F32, name="scale")
+        wa_raw = keep.tile([P, 2, QL], I32, align_bytes=64, name="wa_raw")
+        wa = keep.tile([P, 2, QL], I32, align_bytes=64, name="wa")
+        wb = keep.tile([P, 2, H * ND], I32, align_bytes=64, name="wb")
+        planes = keep.tile([P, QL], U8, align_bytes=64, name="planes")
+        wa_s = keep.tile([P, QL], U8, align_bytes=64, name="wa_s")
+        wb_s = keep.tile([P, 2, H * ND], U8, align_bytes=64, name="wb_s")
+        mark = keep.tile([P, 2], BF16, name="mark")
+        mark2 = keep.tile([P, 2], F32, name="mark2")
+        pos = keep.tile([P, GROUPS * J], F32, name="pos")
+        turns = keep.tile([P, GROUPS * J, HALF], F32, name="turns")
+        whole_i = keep.tile([P, GROUPS * J, HALF], I32, name="whole_i")
+        whole = keep.tile([P, GROUPS * J, HALF], F32, name="whole")
+        frac = keep.tile([P, GROUPS * J, HALF], F32, name="frac")
+        fold = keep.tile([P, 3, GROUPS * J * HALF], F32, name="fold")
+        fold2 = keep.tile([P, 3 * GROUPS * J * HALF], F32, name="fold2")
+        trig = keep.tile([P, 3, GROUPS * J, HALF], F32, name="trig")
+
+        state = {}
+
+        def load(g):
+            xt = xin.tile([P, B, J * D], U8, name="xt")
+            nc.sync.dma_start(out=xt[:], in_=x_view[g])
+            state["xt", g] = xt
+
+        def widen(g, tile):
+            if tile == 0:
+                xs_new = work.tile([P, TILES, D], BF16, align_bytes=64, name="xs")
+                state["xs", g] = xs_new
+            xs = state["xs", g]
+            b, j = divmod(tile, J)
+            nc.vector.tensor_tensor(
+                out=xs[:, tile, :],
+                in0=state["xt", g][:, b, j * D : (j + 1) * D].bitcast(FP8),
+                in1=scale[:],
+                op=MULT,
+            )
+
+        def turn(g, pair):
+            if pair == 0:
+                xg_new = work.tile([P, 2, TOK * 4], BF16, align_bytes=64, name="xg")
+                state["xg", g] = xg_new
+            xg, xs = state["xg", g], state["xs", g]
+            for kp in range(2):
+                tp = ps_t.tile([P, 2, 2, P], F32, name="tp")
+                for a in range(2):
+                    words = xs[:, 2 * pair + a, :].bitcast(F32)
+                    for u in range(2):
+                        nc.tensor.transpose(
+                            tp[:, a, u, :], words[:, 256 * kp + u : 256 * (kp + 1) : 2], ident[:]
+                        )
+                dst = xg[:, kp, 1024 * pair : 1024 * (pair + 1)].bitcast(F32)
+                nc.scalar.copy(
+                    out=dst.rearrange("p (a r u) -> p a r u", a=2, u=2),
+                    in_=tp[:].rearrange("p a u r -> p a r u"),
+                )
+
+        def quant_x(g):
+            xq = work.tile([P, 2, TOK], I32, align_bytes=64, name="xq")
+            xq_s = work.tile([P, 2, TOK], U8, align_bytes=64, name="xq_s")
+            state["xq", g], state["xq_s", g] = xq, xq_s
+            for kp in range(2):
+                nc.vector.quantize_mx(
+                    out=xq[:, kp, :].bitcast(FP8X4), scales=xq_s[:, kp, :], in_=state["xg", g][:, kp, :]
+                )
+
+        def project_a(g):
+            xq, xq_s = state["xq", g], state["xq_s", g]
+            qg = work.tile([P, TOK * 4], BF16, align_bytes=64, name="qg")
+            state["qg", g] = qg
+            for tile in range(TILES):
+                cols = slice(tile * P, (tile + 1) * P)
+                ql = ps_l.tile([P, 4, P], F32, name="ql")
+                for t in range(4):
+                    ch = slice(t * P, (t + 1) * P)
+                    for kp in range(2):
+                        nc.tensor.matmul_mx(
+                            out=ql[:, t, :],
+                            lhsT=wa[:, kp, ch].bitcast(FP8X4),
+                            lhsT_scale=wa_s[4 * kp :, ch],
+                            rhs=xq[:, kp, cols].bitcast(FP8X4),
+                            rhs_scale=xq_s[:, kp, cols],
+                            start=(kp == 0),
+                            stop=(kp == 1),
+                        )
+                nc.scalar.copy(
+                    out=qg[:, 512 * tile : 512 * (tile + 1)].rearrange("p (n t) -> p n t", t=4),
+                    in_=ql[:].rearrange("p t n -> p n t"),
+                )
+
+        def quant_q(g):
+            qq = work.tile([P, TOK], I32, align_bytes=64, name="qq")
+            qq_s = work.tile([P, TOK], U8, align_bytes=64, name="qq_s")
+            state["qq", g], state["qq_s", g] = qq, qq_s
+            nc.vector.quantize_mx(out=qq[:].bitcast(FP8X4), scales=qq_s[:], in_=state["qg", g][:])
+
+        def project_b(g, part, j):
+            qq, qq_s = state["qq", g], state["qq_s", g]
+            if part == 1:
+                bank = ps_p.tile([P, B, H * RD], F32, name="qp")
+                state["qp", g, j] = bank
+            else:
+                bank = ps_n.tile([P, B, H * ND], F32, name="qn")
+            for b in range(B):
+                tile = b * J + j
+                cols = slice(tile * P, (tile + 1) * P)
+                nc.tensor.matmul_mx(
+                    out=bank[:, b, :],
+                    lhsT=qq[:, cols].bitcast(FP8X4),
+                    lhsT_scale=qq_s[:, cols],
+                    rhs=wb[:, part, :].bitcast(FP8X4),
+                    rhs_scale=wb_s[8:, part, :],
+                    start=True,
+                    stop=True,
+                )
+            if part == 0:
+                nc.scalar.copy(
+                    out=state["ot", g][:, :, j, 0:ND], in_=bank[:].rearrange("p b (h d) -> p (b h) d", d=ND)
+                )
+
+        def rotate(g, j):
+            gj = g * J + j
+            qp = state["qp", g, j][:].rearrange("p b (h i e) -> p (b h) i e", h=H, e=2)
+            shape = [P, B * H, HALF, 2]
+            t1 = prod.tile([P, B * H, HALF, 2], F32, name="t1")
+            t2 = prod.tile([P, B * H, HALF, 2], F32, name="t2")
+            cos = trig[:, 0, gj, :].unsqueeze(1).unsqueeze(3).to_broadcast(shape)
+            sin = trig[:, 1:3, gj, :].rearrange("p e i -> p i e").unsqueeze(1).to_broadcast(shape)
+            nc.vector.tensor_tensor(out=t1[:], in0=qp, in1=cos, op=MULT)
+            nc.vector.tensor_tensor(out=t2[:], in0=qp[:, :, :, ::-1], in1=sin, op=MULT)
+            state["t", g, j] = (t1, t2)
+
+        def add_rotated(engine, g, j):
+            t1, t2 = state["t", g, j]
+            engine.tensor_tensor(
+                out=state["ot", g][:, :, j, ND:HD],
+                in0=t1[:].rearrange("p q i e -> p q (i e)"),
+                in1=t2[:].rearrange("p q i e -> p q (i e)"),
+                op=ADD,
+            )
+
+        def store(g):
+            nc.sync.dma_start(
+                out=out_view[g], in_=state["ot", g][:].rearrange("p q j d -> p q (j d)")
+            )
+
+        with tc.manual_schedule():
+            load(0)
+            row = x_scale.rearrange("o q k -> (o q k)").partition_broadcast(P)
+            nc.scalar.dma_start(out=scale[:], in_=row)
+            nc.vector.memset(planes[:].bitcast(I32), 0)
+            nc.sync.dma_start(
+                out=wa_raw[:], in_=wqa_words.rearrange("g p n t -> p g (n t)").bitcast(I32)
+            )
+            for q in range(4):
+                nc.sync.dma_start(
+                    out=planes[32 * q : 32 * q + 8, :].bitcast(I32),
+                    in_=wqa_scales[:, 4 * q : 4 * q + 4, :].bitcast(I32),
+                )
+            for q in range(4):
+                nc.sync.dma_start(
+                    out=planes[32 * q + 8 : 32 * q + 12, :].bitcast(I32),
+                    in_=wqb_scales[0, 4 * q : 4 * q + 4, :].bitcast(I32),
+                )
+            wb_view = wqb_words.rearrange("o p (h c i) t -> c p (o h) (i t)", h=H, c=2)
+            for part in range(2):
+                nc.sync.dma_start(
+                    out=wb[:, part, :].rearrange("p (h i) -> p h i", h=H), in_=wb_view[part].bitcast(I32)
+                )
+            load(1)
+            load(2)
+
+            make_identity(nc, ident[:])
+            nc.gpsimd.iota(
+                pos[:], pattern=[[P * J, GROUPS], [1, J]], base=0, channel_multiplier=J,
+                allow_small_or_imprecise_dtypes=True,
+            )
+            for i in range(HALF):
+                per_turn = 10000.0 ** (-2.0 * i / RD) / (2.0 * math.pi)
+                nc.gpsimd.tensor_scalar(
+                    out=turns[:, :, i], in0=pos[:], scalar1=per_turn, scalar2=None, op0=MULT
+                )
+
+            def tables_vector():
+                nc.vector.tensor_copy(out=whole_i[:], in_=turns[:])
+                nc.vector.tensor_copy(out=whole[:], in_=whole_i[:])
+                nc.vector.tensor_tensor(out=frac[:], in0=turns[:], in1=whole[:], op=SUB)
+
+            def tables_scalar():
+                for n, shift in enumerate((0.0, 0.25, -0.25)):
+                    nc.scalar.activation(
+                        out=fold[:, n, :], in_=frac[:].rearrange("p g i -> p (g i)"), func=AF.Abs, bias=shift
+                    )
+                nc.scalar.activation(
+                    out=fold2[:], in_=fold[:].rearrange("p n q -> p (n q)"), func=AF.Abs, bias=-0.5
+                )
+                nc.scalar.activation(
+                    out=trig[:].rearrange("p n g i -> p (n g i)"), in_=fold2[:], func=AF.Sin,
+                    bias=-0.5 * math.pi, scale=2.0 * math.pi,
+                )
+
+            def weights():
+                nc.vector.tensor_copy(
+                    out=wa[:].rearrange("p g (t m) -> p g t m", t=4),
+                    in_=wa_raw[:].rearrange("p g (m t) -> p g t m", t=4),
+                )
+                nc.vector.tensor_copy(
+                    out=wa_s[:].rearrange("p (t m) -> p t m", t=4),
+                    in_=planes[:].rearrange("p (m t) -> p t m", t=4),
+                )
+                nc.vector.tensor_copy(
+                    out=wb_s[:].rearrange("p c (h i) -> p c h i", h=H),
+                    in_=planes[:].rearrange("p (h c i) -> p c h i", h=H, c=2),
+                )
+
+            for s in range(GROUPS + 3):
+                if s < GROUPS and s > 0 and s + 2 < GROUPS:
+                    load(s + 2)
+                if s == 1:
+                    weights()
+                    tables_vector()
+                early = s <= GROUPS
+                g = s - 4
+                if 0 <= g and early:
+                    nc.gpsimd.tensor_copy(out=mark[:], in_=state["xs", s - 1][:, 3, 0:2])
+                    add_rotated(nc.gpsimd, g, 0)
+                    add_rotated(nc.gpsimd, g, 1)
+                    store(g)
+                if 0 <= s - 3:
+                    rotate(s - 3, 0)
+                    rotate(s - 3, 1)
+                if 0 <= g and not early:
+                    nc.gpsimd.tensor_copy(out=mark2[:], in_=state["t", s - 3, 0][0][:, 0, 0, :])
+                    add_rotated(nc.gpsimd, g, 0)
+                    add_rotated(nc.gpsimd, g, 1)
+                    store(g)
+                if 0 <= s - 2 < GROUPS:
+                    c = s - 2
+                    ot = outs.tile([P, B * H, J, HD], F32, name="ot")
+                    state["ot", c] = ot
+                    quant_q(c)
+                    for part in (1, 0):
+                        for j in range(J):
+                            project_b(c, part, j)
+                if 0 <= s - 1 < GROUPS:
+                    quant_x(s - 1)
+                    project_a(s - 1)
+                if s == 1:
+                    tables_scalar()
+                if s < GROUPS:
+                    for pair in range(2):
+                        widen(s, 2 * pair)
+                        widen(s, 2 * pair + 1)
+                        turn(s, pair)
+            add_rotated(nc.vector, GROUPS - 1, 0)
+            add_rotated(nc.vector, GROUPS - 1, 1)
+            store(GROUPS - 1)

@@ -13,6 +13,7 @@ J = 2
 TILES = B * J
 TOK = TILES * P
 HALF = RD // 2
+SCALAR_GROUPS = ()
 FLOPS = 2 * B * S * QL * (D + H * HD)
 
 F32 = mybir.dt.float32
@@ -34,8 +35,8 @@ def tile_mlaattention_pa_t_w8_kernel(
     with ExitStack() as ctx:
         keep = ctx.enter_context(tc.tile_pool(name="keep", bufs=1))
         xin = ctx.enter_context(tc.tile_pool(name="xin", bufs=3))
+        mid = ctx.enter_context(tc.tile_pool(name="mid", bufs=3))
         work = ctx.enter_context(tc.tile_pool(name="work", bufs=2))
-        prod = ctx.enter_context(tc.tile_pool(name="prod", bufs=4))
         outs = ctx.enter_context(tc.tile_pool(name="outs", bufs=4))
         ps_t = ctx.enter_context(tc.psum_pool(name="ps_t", bufs=2))
         ps_l = ctx.enter_context(tc.psum_pool(name="ps_l", bufs=2))
@@ -43,10 +44,11 @@ def tile_mlaattention_pa_t_w8_kernel(
         ps_p = ctx.enter_context(tc.psum_pool(name="ps_p", bufs=2))
 
         x_view = x_bytes.rearrange("b (g p j) k -> g p b (j k)", p=P, j=J)
-        out_view = out.rearrange("b h (g p j) d -> g p (b h) (j d)", p=P, j=J)
+        out_view = out.rearrange("b h (g p j) d -> g p (b h) j d", p=P, j=J)
 
         ident = keep.tile([P, P], F32, name="ident")
         scale = keep.tile([P, D], F32, name="scale")
+        scale_col = keep.tile([P, 2, 4], F32, name="scale_col")
         wa_raw = keep.tile([P, 2, QL], I32, align_bytes=64, name="wa_raw")
         wa = keep.tile([P, 2, QL], I32, align_bytes=64, name="wa")
         wb = keep.tile([P, 2, H * ND], I32, align_bytes=64, name="wb")
@@ -54,7 +56,6 @@ def tile_mlaattention_pa_t_w8_kernel(
         wa_s = keep.tile([P, QL], U8, align_bytes=64, name="wa_s")
         wb_s = keep.tile([P, 2, H * ND], U8, align_bytes=64, name="wb_s")
         mark = keep.tile([P, 2], BF16, name="mark")
-        mark2 = keep.tile([P, 2], F32, name="mark2")
         pos = keep.tile([P, GROUPS * J], F32, name="pos")
         turns = keep.tile([P, GROUPS * J, HALF], F32, name="turns")
         whole_i = keep.tile([P, GROUPS * J, HALF], I32, name="whole_i")
@@ -71,36 +72,50 @@ def tile_mlaattention_pa_t_w8_kernel(
             nc.sync.dma_start(out=xt[:], in_=x_view[g])
             state["xt", g] = xt
 
-        def widen(g, tile):
-            if tile == 0:
-                xs_new = work.tile([P, TILES, D], BF16, align_bytes=64, name="xs")
-                state["xs", g] = xs_new
-            xs = state["xs", g]
+        def widen(g, tile, k0, k1):
             b, j = divmod(tile, J)
             nc.vector.tensor_tensor(
-                out=xs[:, tile, :],
-                in0=state["xt", g][:, b, j * D : (j + 1) * D].bitcast(FP8),
-                in1=scale[:],
+                out=state["xs", g][:, tile, k0:k1],
+                in0=state["xt", g][:, b, j * D + k0 : j * D + k1].bitcast(FP8),
+                in1=scale[:, k0:k1],
                 op=MULT,
             )
 
-        def turn(g, pair):
-            if pair == 0:
-                xg_new = work.tile([P, 2, TOK * 4], BF16, align_bytes=64, name="xg")
-                state["xg", g] = xg_new
-            xg, xs = state["xg", g], state["xs", g]
-            for kp in range(2):
-                tp = ps_t.tile([P, 2, 2, P], F32, name="tp")
-                for a in range(2):
-                    words = xs[:, 2 * pair + a, :].bitcast(F32)
-                    for u in range(2):
-                        nc.tensor.transpose(
-                            tp[:, a, u, :], words[:, 256 * kp + u : 256 * (kp + 1) : 2], ident[:]
-                        )
-                dst = xg[:, kp, 1024 * pair : 1024 * (pair + 1)].bitcast(F32)
+        def cast(g, tile, k0, k1):
+            b, j = divmod(tile, J)
+            nc.scalar.copy(
+                out=state["xs", g][:, tile, k0:k1],
+                in_=state["xt", g][:, b, j * D + k0 : j * D + k1].bitcast(FP8),
+            )
+
+        def turn(g, pair, kp, scaled):
+            xs = state["xs", g]
+            dst = state["xg", g][:, kp, 1024 * pair : 1024 * (pair + 1)]
+            tp = ps_t.tile([P, 2, 2, P], F32, name="tp")
+            for a in range(2):
+                words = xs[:, 2 * pair + a, :].bitcast(F32)
+                for u in range(2):
+                    nc.tensor.transpose(
+                        tp[:, a, u, :], words[:, 256 * kp + u : 256 * (kp + 1) : 2], ident[:]
+                    )
+            if scaled:
                 nc.scalar.copy(
-                    out=dst.rearrange("p (a r u) -> p a r u", a=2, u=2),
+                    out=dst.bitcast(F32).rearrange("p (a r u) -> p a r u", a=2, u=2),
                     in_=tp[:].rearrange("p a u r -> p a r u"),
+                )
+            else:
+                planar = work.tile([P, 4, 2 * P], BF16, name="planar")
+                halves = tp[:].rearrange("p a u r -> p (a u r)").bitcast(BF16)
+                halves = halves.rearrange("p (a u r e) -> p a u r e", a=2, u=2, e=2)
+                for t in range(4):
+                    nc.scalar.activation(
+                        out=planar[:, t, :].rearrange("p (a r) -> p a r", a=2),
+                        in_=halves[:, :, t // 2, :, t % 2],
+                        func=AF.Copy,
+                        scale=scale_col[:, kp, t : t + 1],
+                    )
+                nc.scalar.copy(
+                    out=dst.rearrange("p (n t) -> p n t", t=4), in_=planar[:].rearrange("p t n -> p n t")
                 )
 
         def quant_x(g):
@@ -170,8 +185,8 @@ def tile_mlaattention_pa_t_w8_kernel(
             gj = g * J + j
             qp = state["qp", g, j][:].rearrange("p b (h i e) -> p (b h) i e", h=H, e=2)
             shape = [P, B * H, HALF, 2]
-            t1 = prod.tile([P, B * H, HALF, 2], F32, name="t1")
-            t2 = prod.tile([P, B * H, HALF, 2], F32, name="t2")
+            t1 = work.tile([P, B * H, HALF, 2], F32, bufs=4, name="t1")
+            t2 = work.tile([P, B * H, HALF, 2], F32, bufs=4, name="t2")
             cos = trig[:, 0, gj, :].unsqueeze(1).unsqueeze(3).to_broadcast(shape)
             sin = trig[:, 1:3, gj, :].rearrange("p e i -> p i e").unsqueeze(1).to_broadcast(shape)
             nc.vector.tensor_tensor(out=t1[:], in0=qp, in1=cos, op=MULT)
@@ -189,14 +204,19 @@ def tile_mlaattention_pa_t_w8_kernel(
 
         def store(g):
             nc.sync.dma_start(
-                out=out_view[g], in_=state["ot", g][:].rearrange("p q j d -> p q (j d)")
+                out=out_view[g].rearrange("p q j d -> p q (j d)"),
+                in_=state["ot", g][:].rearrange("p q j d -> p q (j d)"),
             )
 
         with tc.manual_schedule():
-            load(0)
-            row = x_scale.rearrange("o q k -> (o q k)").partition_broadcast(P)
-            nc.scalar.dma_start(out=scale[:], in_=row)
             nc.vector.memset(planes[:].bitcast(I32), 0)
+            nc.gpsimd.iota(
+                pos[:], pattern=[[P * J, GROUPS], [1, J]], base=0, channel_multiplier=J,
+                allow_small_or_imprecise_dtypes=True,
+            )
+            make_identity(nc, ident[:])
+            load(0)
+            nc.scalar.dma_start(out=scale[:], in_=x_scale.rearrange("o q k -> (o q k)").partition_broadcast(P))
             nc.sync.dma_start(
                 out=wa_raw[:], in_=wqa_words.rearrange("g p n t -> p g (n t)").bitcast(I32)
             )
@@ -210,96 +230,82 @@ def tile_mlaattention_pa_t_w8_kernel(
                     out=planes[32 * q + 8 : 32 * q + 12, :].bitcast(I32),
                     in_=wqb_scales[0, 4 * q : 4 * q + 4, :].bitcast(I32),
                 )
+
+            load(1)
             wb_view = wqb_words.rearrange("o p (h c i) t -> c p (o h) (i t)", h=H, c=2)
             for part in range(2):
                 nc.sync.dma_start(
                     out=wb[:, part, :].rearrange("p (h i) -> p h i", h=H), in_=wb_view[part].bitcast(I32)
                 )
-            load(1)
-            load(2)
 
-            make_identity(nc, ident[:])
-            nc.gpsimd.iota(
-                pos[:], pattern=[[P * J, GROUPS], [1, J]], base=0, channel_multiplier=J,
-                allow_small_or_imprecise_dtypes=True,
-            )
             for i in range(HALF):
                 per_turn = 10000.0 ** (-2.0 * i / RD) / (2.0 * math.pi)
-                nc.gpsimd.tensor_scalar(
+                nc.vector.tensor_scalar(
                     out=turns[:, :, i], in0=pos[:], scalar1=per_turn, scalar2=None, op0=MULT
                 )
+            nc.vector.tensor_copy(out=whole_i[:], in_=turns[:])
+            nc.vector.tensor_copy(out=whole[:], in_=whole_i[:])
+            nc.vector.tensor_tensor(out=frac[:], in0=turns[:], in1=whole[:], op=SUB)
+            for n, shift in enumerate((0.0, 0.25, -0.25)):
+                nc.scalar.activation(
+                    out=fold[:, n, :], in_=frac[:].rearrange("p g i -> p (g i)"), func=AF.Abs, bias=shift
+                )
+            nc.scalar.activation(
+                out=fold2[:], in_=fold[:].rearrange("p n q -> p (n q)"), func=AF.Abs, bias=-0.5
+            )
+            nc.scalar.activation(
+                out=trig[:].rearrange("p n g i -> p (n g i)"), in_=fold2[:], func=AF.Sin,
+                bias=-0.5 * math.pi, scale=2.0 * math.pi,
+            )
 
-            def tables_vector():
-                nc.vector.tensor_copy(out=whole_i[:], in_=turns[:])
-                nc.vector.tensor_copy(out=whole[:], in_=whole_i[:])
-                nc.vector.tensor_tensor(out=frac[:], in0=turns[:], in1=whole[:], op=SUB)
-
-            def tables_scalar():
-                for n, shift in enumerate((0.0, 0.25, -0.25)):
-                    nc.scalar.activation(
-                        out=fold[:, n, :], in_=frac[:].rearrange("p g i -> p (g i)"), func=AF.Abs, bias=shift
+            for s in range(GROUPS + 4):
+                if s < GROUPS:
+                    xs = work.tile([P, TILES, D], BF16, align_bytes=64, name="xs")
+                    xg = mid.tile([P, 2, TOK * 4], BF16, align_bytes=64, name="xg")
+                    state["xs", s], state["xg", s] = xs, xg
+                    if s + 2 < GROUPS:
+                        load(s + 2)
+                if s in SCALAR_GROUPS:
+                    for tile in range(2):
+                        cast(s, tile, 512, D)
+                if s == 2:
+                    nc.vector.tensor_copy(
+                        out=wa[:].rearrange("p g (t m) -> p g t m", t=4),
+                        in_=wa_raw[:].rearrange("p g (m t) -> p g t m", t=4),
                     )
-                nc.scalar.activation(
-                    out=fold2[:], in_=fold[:].rearrange("p n q -> p (n q)"), func=AF.Abs, bias=-0.5
-                )
-                nc.scalar.activation(
-                    out=trig[:].rearrange("p n g i -> p (n g i)"), in_=fold2[:], func=AF.Sin,
-                    bias=-0.5 * math.pi, scale=2.0 * math.pi,
-                )
-
-            def weights():
-                nc.vector.tensor_copy(
-                    out=wa[:].rearrange("p g (t m) -> p g t m", t=4),
-                    in_=wa_raw[:].rearrange("p g (m t) -> p g t m", t=4),
-                )
-                nc.vector.tensor_copy(
-                    out=wa_s[:].rearrange("p (t m) -> p t m", t=4),
-                    in_=planes[:].rearrange("p (m t) -> p t m", t=4),
-                )
-                nc.vector.tensor_copy(
-                    out=wb_s[:].rearrange("p c (h i) -> p c h i", h=H),
-                    in_=planes[:].rearrange("p (h c i) -> p c h i", h=H, c=2),
-                )
-
-            for s in range(GROUPS + 3):
-                if s < GROUPS and s > 0 and s + 2 < GROUPS:
-                    load(s + 2)
-                if s == 1:
-                    weights()
-                    tables_vector()
-                early = s <= GROUPS
-                g = s - 4
-                if 0 <= g and early:
-                    nc.gpsimd.tensor_copy(out=mark[:], in_=state["xs", s - 1][:, 3, 0:2])
-                    add_rotated(nc.gpsimd, g, 0)
-                    add_rotated(nc.gpsimd, g, 1)
-                    store(g)
-                if 0 <= s - 3:
-                    rotate(s - 3, 0)
-                    rotate(s - 3, 1)
-                if 0 <= g and not early:
-                    nc.gpsimd.tensor_copy(out=mark2[:], in_=state["t", s - 3, 0][0][:, 0, 0, :])
-                    add_rotated(nc.gpsimd, g, 0)
-                    add_rotated(nc.gpsimd, g, 1)
-                    store(g)
+                    nc.vector.tensor_copy(
+                        out=wa_s[:].rearrange("p (t m) -> p t m", t=4),
+                        in_=planes[:].rearrange("p (m t) -> p t m", t=4),
+                    )
+                    nc.vector.tensor_copy(
+                        out=wb_s[:].rearrange("p c (h i) -> p c h i", h=H),
+                        in_=planes[:].rearrange("p (h c i) -> p c h i", h=H, c=2),
+                    )
                 if 0 <= s - 2 < GROUPS:
-                    c = s - 2
+                    quant_x(s - 2)
+                    project_a(s - 2)
+                if 0 <= s - 4:
+                    rotate(s - 4, 0)
+                    rotate(s - 4, 1)
+                if 0 <= s - 3 < GROUPS:
                     ot = outs.tile([P, B * H, J, HD], F32, name="ot")
-                    state["ot", c] = ot
-                    quant_q(c)
+                    state["ot", s - 3] = ot
+                    quant_q(s - 3)
                     for part in (1, 0):
                         for j in range(J):
-                            project_b(c, part, j)
-                if 0 <= s - 1 < GROUPS:
-                    quant_x(s - 1)
-                    project_a(s - 1)
-                if s == 1:
-                    tables_scalar()
+                            project_b(s - 3, part, j)
+                if 0 <= s - 4:
+                    add_rotated(nc.vector, s - 4, 0)
+                    add_rotated(nc.vector, s - 4, 1)
+                    store(s - 4)
                 if s < GROUPS:
                     for pair in range(2):
-                        widen(s, 2 * pair)
-                        widen(s, 2 * pair + 1)
-                        turn(s, pair)
-            add_rotated(nc.vector, GROUPS - 1, 0)
-            add_rotated(nc.vector, GROUPS - 1, 1)
-            store(GROUPS - 1)
+                        on_scalar = s in SCALAR_GROUPS and pair == 0
+                        for tile in (2 * pair, 2 * pair + 1):
+                            widen(s, tile, 0, 512 if on_scalar else D)
+                        if on_scalar:
+                            turn(s, pair, 1, False)
+                            turn(s, pair, 0, True)
+                        else:
+                            turn(s, pair, 0, True)
+                            turn(s, pair, 1, True)

@@ -7,13 +7,19 @@ from concourse.masks import make_identity
 B, S, D, QL = 2, 2048, 1024, 512
 H, ND, RD = 4, 64, 64
 HD = ND + RD
+HALF = RD // 2
 P = 128
-GROUPS = 8
 J = 2
 TILES = B * J
 TOK = TILES * P
-HALF = RD // 2
-SCALAR_GROUPS = ()
+GROUPS = B * S // TOK
+PAIR = 2 * P
+PACK = 4
+KP = D // (P * PACK)
+K_PASS = P * PACK
+PAIRS = H * HALF
+SLOTS = GROUPS * J
+LAST_STORES = 4
 FLOPS = 2 * B * S * QL * (D + H * HD)
 
 F32 = mybir.dt.float32
@@ -22,10 +28,18 @@ I32 = mybir.dt.int32
 U8 = mybir.dt.uint8
 FP8 = mybir.dt.float8_e4m3fn
 FP8X4 = mybir.dt.float8_e4m3fn_x4
-MULT = mybir.AluOpType.mult
-ADD = mybir.AluOpType.add
-SUB = mybir.AluOpType.subtract
+ALU = mybir.AluOpType
 AF = mybir.ActivationFunctionType
+
+SCALAR_GROUPS = (1, 3, 4, 6)
+
+ORDER = """
+f K1 B00 B01 t0 B02 B03 T00 W B10 t1 B11 T01 t2 B12 T10 D0 A00 B13 B20 B21 T11 B22 A01 K3 D1 T20 B23 A10 B30 B31
+T21 F0 B32 A11 T30 S0 E00 N00 E01 B33 D2 B40 T31 F1 B41 B42 B43 M0 B50 B51 N01 B52 K4 D3 R0 A20 N10 A21 T40 S1
+A30 E10 F2 E11 T41 N11 M1 A31 N20 B53 B60 K6 B61 D4 T50 B62 E20 A40 N21 T51 B63 E21 F3 B70 S2 N30 R1 A41 T60 M2
+N31 E30 E31 D5 S3 F4 B71 M3 B72 A50 T61 E40 N40 R2 D6 A51 T70 S4 N41 E41 B73 A60 T71 F5 M4 R3 N50 A61 E50 N51
+E51 S5 D7 A70 R4 F6 M5 N60 S6 E60 E61 M6 R5 A71 N61 F7 S7 E70 R6 N70 E71 M7 N71 R7
+"""
 
 
 def tile_mlaattention_pa_t_w8_kernel(
@@ -34,278 +48,327 @@ def tile_mlaattention_pa_t_w8_kernel(
     nc = tc.nc
     with ExitStack() as ctx:
         keep = ctx.enter_context(tc.tile_pool(name="keep", bufs=1))
-        xin = ctx.enter_context(tc.tile_pool(name="xin", bufs=3))
-        mid = ctx.enter_context(tc.tile_pool(name="mid", bufs=3))
+        xin = ctx.enter_context(tc.tile_pool(name="xin", bufs=4))
+        turned = ctx.enter_context(tc.tile_pool(name="turned", bufs=3))
         work = ctx.enter_context(tc.tile_pool(name="work", bufs=2))
         outs = ctx.enter_context(tc.tile_pool(name="outs", bufs=4))
-        ps_t = ctx.enter_context(tc.psum_pool(name="ps_t", bufs=2))
-        ps_l = ctx.enter_context(tc.psum_pool(name="ps_l", bufs=2))
-        ps_n = ctx.enter_context(tc.psum_pool(name="ps_n", bufs=2))
-        ps_p = ctx.enter_context(tc.psum_pool(name="ps_p", bufs=2))
+        ps_turn = ctx.enter_context(tc.psum_pool(name="ps_turn", bufs=2))
+        ps_latent = ctx.enter_context(tc.psum_pool(name="ps_latent", bufs=2))
+        ps_rot = ctx.enter_context(tc.psum_pool(name="ps_rot", bufs=2))
+        ps_sum = ctx.enter_context(tc.psum_pool(name="ps_sum", bufs=1))
+        ps_plain = ctx.enter_context(tc.psum_pool(name="ps_plain", bufs=1))
 
         x_view = x_bytes.rearrange("b (g p j) k -> g p b (j k)", p=P, j=J)
-        out_view = out.rearrange("b h (g p j) d -> g p (b h) j d", p=P, j=J)
+        out_view = out.rearrange("b h (g p j) d -> g p (b h) (j d)", p=P, j=J)
 
-        ident = keep.tile([P, P], F32, name="ident")
-        scale = keep.tile([P, D], F32, name="scale")
-        scale_col = keep.tile([P, 2, 4], F32, name="scale_col")
-        wa_raw = keep.tile([P, 2, QL], I32, align_bytes=64, name="wa_raw")
-        wa = keep.tile([P, 2, QL], I32, align_bytes=64, name="wa")
+        identity = keep.tile([P, P], F32, name="identity")
+        scale_row = keep.tile([P, D], F32, name="scale_row")
+        scale_col = keep.tile([P, KP, PACK], F32, name="scale_col")
+        wa_raw = keep.tile([P, KP, QL], I32, align_bytes=64, name="wa_raw")
+        wa = keep.tile([P, KP, QL], I32, align_bytes=64, name="wa")
+        wb_raw = keep.tile([P, H * HD], I32, align_bytes=64, name="wb_raw")
         wb = keep.tile([P, 2, H * ND], I32, align_bytes=64, name="wb")
         planes = keep.tile([P, QL], U8, align_bytes=64, name="planes")
         wa_s = keep.tile([P, QL], U8, align_bytes=64, name="wa_s")
         wb_s = keep.tile([P, 2, H * ND], U8, align_bytes=64, name="wb_s")
-        mark = keep.tile([P, 2], BF16, name="mark")
-        pos = keep.tile([P, GROUPS * J], F32, name="pos")
-        turns = keep.tile([P, GROUPS * J, HALF], F32, name="turns")
-        whole_i = keep.tile([P, GROUPS * J, HALF], I32, name="whole_i")
-        whole = keep.tile([P, GROUPS * J, HALF], F32, name="whole")
-        frac = keep.tile([P, GROUPS * J, HALF], F32, name="frac")
-        fold = keep.tile([P, 3, GROUPS * J * HALF], F32, name="fold")
-        fold2 = keep.tile([P, 3 * GROUPS * J * HALF], F32, name="fold2")
-        trig = keep.tile([P, 3, GROUPS * J, HALF], F32, name="trig")
+        pos = keep.tile([P, SLOTS], F32, name="pos")
+        freq = keep.tile([P, HALF], F32, name="freq")
+        turns = keep.tile([P, SLOTS, HALF], F32, name="turns")
+        whole_i = keep.tile([P, SLOTS, HALF], I32, name="whole_i")
+        whole = keep.tile([P, SLOTS, HALF], F32, name="whole")
+        frac = keep.tile([P, SLOTS, HALF], F32, name="frac")
+        fold = keep.tile([P, 3, SLOTS, HALF], F32, name="fold")
+        trig = keep.tile([P, 3, SLOTS, HALF], F32, name="trig")
+        cross = keep.tile([P, 2, SLOTS, HALF], F32, name="cross")
 
-        state = {}
+        held = {}
 
         def load(g):
-            xt = xin.tile([P, B, J * D], U8, name="xt")
-            nc.sync.dma_start(out=xt[:], in_=x_view[g])
-            state["xt", g] = xt
+            held["bytes", g] = xin.tile([P, B, J * D], U8, name="x_tile")
+            nc.sync.dma_start(out=held["bytes", g][:], in_=x_view[g])
 
-        def widen(g, tile, k0, k1):
+        def open_group(g):
+            if ("wide", g) not in held:
+                held["wide", g] = work.tile([P, TILES, D], BF16, align_bytes=64, name="wide")
+                held["turned", g] = turned.tile([P, KP, TOK * PACK], BF16, align_bytes=64, name="turned_x")
+
+        def split(g, tile):
+            return KP - 1 if g in SCALAR_GROUPS and tile < J else KP
+
+        def fp8_view(g, tile, k0, k1):
             b, j = divmod(tile, J)
+            return held["bytes", g][:, b, j * D + k0 : j * D + k1].bitcast(FP8)
+
+        def widen_plain(g):
+            open_group(g)
+            for tile in range(J):
+                k0 = split(g, tile) * K_PASS
+                nc.scalar.copy(out=held["wide", g][:, tile, k0:D], in_=fp8_view(g, tile, k0, D))
+
+        def widen(g, tile):
+            open_group(g)
+            k1 = split(g, tile) * K_PASS
             nc.vector.tensor_tensor(
-                out=state["xs", g][:, tile, k0:k1],
-                in0=state["xt", g][:, b, j * D + k0 : j * D + k1].bitcast(FP8),
-                in1=scale[:, k0:k1],
-                op=MULT,
+                out=held["wide", g][:, tile, 0:k1], in0=fp8_view(g, tile, 0, k1), in1=scale_row[:, 0:k1], op=ALU.mult
             )
+            if tile == TILES - 1 and g + 4 < GROUPS:
+                load(g + 4)
 
-        def cast(g, tile, k0, k1):
-            b, j = divmod(tile, J)
-            nc.scalar.copy(
-                out=state["xs", g][:, tile, k0:k1],
-                in_=state["xt", g][:, b, j * D + k0 : j * D + k1].bitcast(FP8),
-            )
-
-        def turn(g, pair, kp, scaled):
-            xs = state["xs", g]
-            dst = state["xg", g][:, kp, 1024 * pair : 1024 * (pair + 1)]
-            tp = ps_t.tile([P, 2, 2, P], F32, name="tp")
-            for a in range(2):
-                words = xs[:, 2 * pair + a, :].bitcast(F32)
-                for u in range(2):
-                    nc.tensor.transpose(
-                        tp[:, a, u, :], words[:, 256 * kp + u : 256 * (kp + 1) : 2], ident[:]
+        def turn(g, b):
+            for kp in range(KP - 1, -1, -1) if split(g, b * J) < KP else range(KP):
+                bank = ps_turn.tile([P, J, 2, P], F32, name="bank_t")
+                for j in range(J):
+                    words = held["wide", g][:, b * J + j, kp * K_PASS : (kp + 1) * K_PASS].bitcast(F32)
+                    for u in range(2):
+                        nc.tensor.transpose(bank[:, j, u, :], words[:, u::2], identity[:])
+                dst = held["turned", g][:, kp, b * PAIR * PACK : (b + 1) * PAIR * PACK]
+                if kp < split(g, b * J):
+                    nc.scalar.copy(
+                        out=dst.bitcast(F32).rearrange("p (j r u) -> p j r u", j=J, u=2),
+                        in_=bank[:].rearrange("p j u r -> p j r u"),
                     )
-            if scaled:
-                nc.scalar.copy(
-                    out=dst.bitcast(F32).rearrange("p (a r u) -> p a r u", a=2, u=2),
-                    in_=tp[:].rearrange("p a u r -> p a r u"),
-                )
-            else:
-                planar = work.tile([P, 4, 2 * P], BF16, name="planar")
-                halves = tp[:].rearrange("p a u r -> p (a u r)").bitcast(BF16)
-                halves = halves.rearrange("p (a u r e) -> p a u r e", a=2, u=2, e=2)
-                for t in range(4):
-                    nc.scalar.activation(
-                        out=planar[:, t, :].rearrange("p (a r) -> p a r", a=2),
-                        in_=halves[:, :, t // 2, :, t % 2],
-                        func=AF.Copy,
-                        scale=scale_col[:, kp, t : t + 1],
+                else:
+                    planar = work.tile([P, PACK, PAIR], BF16, name="planar")
+                    values = bank[:].rearrange("p j u r -> p (j u r)").bitcast(BF16)
+                    values = values.rearrange("p (j u r e) -> p j u r e", j=J, u=2, e=2)
+                    for t in range(PACK):
+                        u, e = divmod(t, 2)
+                        nc.scalar.activation(
+                            out=planar[:, t, :].rearrange("p (j r) -> p j r", j=J),
+                            in_=values[:, :, u, :, e],
+                            func=AF.Copy,
+                            scale=scale_col[:, kp, t : t + 1],
+                        )
+                    nc.scalar.copy(
+                        out=dst.rearrange("p (n t) -> p n t", t=PACK), in_=planar[:].rearrange("p t n -> p n t")
                     )
-                nc.scalar.copy(
-                    out=dst.rearrange("p (n t) -> p n t", t=4), in_=planar[:].rearrange("p t n -> p n t")
-                )
 
-        def quant_x(g):
-            xq = work.tile([P, 2, TOK], I32, align_bytes=64, name="xq")
-            xq_s = work.tile([P, 2, TOK], U8, align_bytes=64, name="xq_s")
-            state["xq", g], state["xq_s", g] = xq, xq_s
-            for kp in range(2):
+        def quantise_x(g):
+            held["xq", g] = work.tile([P, KP, TOK], I32, align_bytes=64, name="xq")
+            held["xq_s", g] = work.tile([P, KP, TOK], U8, align_bytes=64, name="xq_s")
+            for kp in range(KP):
                 nc.vector.quantize_mx(
-                    out=xq[:, kp, :].bitcast(FP8X4), scales=xq_s[:, kp, :], in_=state["xg", g][:, kp, :]
+                    out=held["xq", g][:, kp, :].bitcast(FP8X4),
+                    scales=held["xq_s", g][:, kp, :],
+                    in_=held["turned", g][:, kp, :],
                 )
 
-        def project_a(g):
-            xq, xq_s = state["xq", g], state["xq_s", g]
-            qg = work.tile([P, TOK * 4], BF16, align_bytes=64, name="qg")
-            state["qg", g] = qg
-            for tile in range(TILES):
-                cols = slice(tile * P, (tile + 1) * P)
-                ql = ps_l.tile([P, 4, P], F32, name="ql")
-                for t in range(4):
-                    ch = slice(t * P, (t + 1) * P)
-                    for kp in range(2):
+        def project_latent(g, half):
+            if half == 0:
+                held["latent", g] = work.tile([P, TOK * PACK], BF16, align_bytes=64, name="latent")
+            for tile in range(half * J, (half + 1) * J):
+                tokens = slice(tile * P, (tile + 1) * P)
+                bank = ps_latent.tile([P, PACK, P], F32, name="bank_l")
+                for t in range(PACK):
+                    channels = slice(t * P, (t + 1) * P)
+                    for kp in range(KP):
                         nc.tensor.matmul_mx(
-                            out=ql[:, t, :],
-                            lhsT=wa[:, kp, ch].bitcast(FP8X4),
-                            lhsT_scale=wa_s[4 * kp :, ch],
-                            rhs=xq[:, kp, cols].bitcast(FP8X4),
-                            rhs_scale=xq_s[:, kp, cols],
+                            out=bank[:, t, :],
+                            lhsT=wa[:, kp, channels].bitcast(FP8X4),
+                            lhsT_scale=wa_s[4 * kp :, channels],
+                            rhs=held["xq", g][:, kp, tokens].bitcast(FP8X4),
+                            rhs_scale=held["xq_s", g][:, kp, tokens],
                             start=(kp == 0),
-                            stop=(kp == 1),
+                            stop=(kp == KP - 1),
                         )
                 nc.scalar.copy(
-                    out=qg[:, 512 * tile : 512 * (tile + 1)].rearrange("p (n t) -> p n t", t=4),
-                    in_=ql[:].rearrange("p t n -> p n t"),
+                    out=held["latent", g][:, tile * P * PACK : (tile + 1) * P * PACK].rearrange(
+                        "p (n t) -> p n t", t=PACK
+                    ),
+                    in_=bank[:].rearrange("p t n -> p n t"),
                 )
 
-        def quant_q(g):
-            qq = work.tile([P, TOK], I32, align_bytes=64, name="qq")
-            qq_s = work.tile([P, TOK], U8, align_bytes=64, name="qq_s")
-            state["qq", g], state["qq_s", g] = qq, qq_s
-            nc.vector.quantize_mx(out=qq[:].bitcast(FP8X4), scales=qq_s[:], in_=state["qg", g][:])
+        def quantise_latent(g):
+            held["lq", g] = work.tile([P, TOK], I32, align_bytes=64, name="lq")
+            held["lq_s", g] = work.tile([P, TOK], U8, align_bytes=64, name="lq_s")
+            nc.vector.quantize_mx(
+                out=held["lq", g][:].bitcast(FP8X4), scales=held["lq_s", g][:], in_=held["latent", g][:]
+            )
 
-        def project_b(g, part, j):
-            qq, qq_s = state["qq", g], state["qq_s", g]
-            if part == 1:
-                bank = ps_p.tile([P, B, H * RD], F32, name="qp")
-                state["qp", g, j] = bank
-            else:
-                bank = ps_n.tile([P, B, H * ND], F32, name="qn")
+        def project_q(g, tile, part, c0, c1, bank, start, stop):
+            tokens = slice(tile * P, (tile + 1) * P)
+            nc.tensor.matmul_mx(
+                out=bank,
+                lhsT=held["lq", g][:, tokens].bitcast(FP8X4),
+                lhsT_scale=held["lq_s", g][:, tokens],
+                rhs=wb[:, part, c0:c1].bitcast(FP8X4),
+                rhs_scale=wb_s[8:, part, c0:c1],
+                start=start,
+                stop=stop,
+            )
+
+        def project_sums(g):
+            bank = ps_sum.tile([P, J, B, PAIRS], F32, name="bank_s")
+            held["sums", g] = bank
+            for j in range(J):
+                for b in range(B):
+                    for e in range(2):
+                        project_q(
+                            g, b * J + j, 1, e * PAIRS, (e + 1) * PAIRS, bank[:, j, b, :], e == 0, e == 1
+                        )
+
+        def project_rotated(g, j):
+            bank = ps_rot.tile([P, 2, B, PAIRS], F32, name="bank_r")
+            held["rot", g, j] = bank
             for b in range(B):
-                tile = b * J + j
-                cols = slice(tile * P, (tile + 1) * P)
-                nc.tensor.matmul_mx(
-                    out=bank[:, b, :],
-                    lhsT=qq[:, cols].bitcast(FP8X4),
-                    lhsT_scale=qq_s[:, cols],
-                    rhs=wb[:, part, :].bitcast(FP8X4),
-                    rhs_scale=wb_s[8:, part, :],
-                    start=True,
-                    stop=True,
+                for e in range(2):
+                    project_q(g, b * J + j, 1, e * PAIRS, (e + 1) * PAIRS, bank[:, e, b, :], True, True)
+
+        def project_plain(g, j):
+            if j == 0:
+                held["out", g] = outs.tile([P, B * H, J, HD], F32, name="out_tile")
+            bank = ps_plain.tile([P, B, H * ND], F32, name="bank_p")
+            for b in range(B):
+                project_q(g, b * J + j, 0, 0, H * ND, bank[:, b, :], True, True)
+            nc.scalar.copy(
+                out=held["out", g][:, :, j, 0:ND], in_=bank[:].rearrange("p b (h d) -> p (b h) d", d=ND)
+            )
+
+        def rotate(g):
+            shared = work.tile([P, J, B * H, HALF], F32, name="shared")
+            other = work.tile([P, J, B * H, HALF, 2], F32, name="other")
+            held["products", g] = (shared, other)
+            nc.vector.tensor_tensor(
+                out=shared[:],
+                in0=held["sums", g][:].rearrange("p j b (h i) -> p j (b h) i", h=H),
+                in1=trig[:, 0, g * J : (g + 1) * J, :].unsqueeze(2).to_broadcast([P, J, B * H, HALF]),
+                op=ALU.mult,
+            )
+            for j in range(J):
+                pairs = held["rot", g, j][:].rearrange("p e b (h i) -> p (b h) i e", h=H)
+                factors = cross[:, :, g * J + j, :].rearrange("p e i -> p i e").unsqueeze(1)
+                nc.vector.tensor_tensor(
+                    out=other[:, j],
+                    in0=pairs[:, :, :, ::-1],
+                    in1=factors.to_broadcast([P, B * H, HALF, 2]),
+                    op=ALU.mult,
                 )
+
+        def add_and_store(g):
+            shared, other = held["products", g]
+            size = B * H // (LAST_STORES if g == GROUPS - 1 else 1)
+            for q0 in range(0, B * H, size):
+                q = slice(q0, q0 + size)
+                nc.vector.tensor_tensor(
+                    out=held["out", g][:, q, :, ND:HD].rearrange("p q j (i e) -> p j q i e", e=2),
+                    in0=shared[:, :, q, :].unsqueeze(4).to_broadcast([P, J, size, HALF, 2]),
+                    in1=other[:, :, q],
+                    op=ALU.add,
+                )
+                nc.sync.dma_start(
+                    out=out_view[g][:, q], in_=held["out", g][:, q].rearrange("p q j d -> p q (j d)")
+                )
+
+        def turn_fractions():
+            nc.vector.tensor_copy(out=whole_i[:], in_=turns[:])
+            nc.vector.tensor_copy(out=whole[:], in_=whole_i[:])
+            nc.vector.tensor_tensor(out=frac[:], in0=turns[:], in1=whole[:], op=ALU.subtract)
+
+        def tables(part):
             if part == 0:
-                nc.scalar.copy(
-                    out=state["ot", g][:, :, j, 0:ND], in_=bank[:].rearrange("p b (h d) -> p (b h) d", d=ND)
+                for n, shift in enumerate((0.0, -0.125, 0.125)):
+                    nc.scalar.activation(out=fold[:, n], in_=frac[:], func=AF.Abs, bias=shift)
+            elif part == 1:
+                nc.scalar.activation(
+                    out=trig[:], in_=fold[:], func=AF.Sin, bias=0.5 * math.pi, scale=-2.0 * math.pi
+                )
+            else:
+                nc.scalar.mul(out=cross[:], in_=trig[:, 1:3], mul=-math.sqrt(2.0))
+
+        def arrange_weights():
+            nc.vector.tensor_copy(
+                out=wa[:].rearrange("p g (t m) -> p g t m", t=PACK),
+                in_=wa_raw[:].rearrange("p g (m t) -> p g t m", t=PACK),
+            )
+            nc.vector.tensor_copy(
+                out=wa_s[:].rearrange("p (t m) -> p t m", t=PACK),
+                in_=planes[:].rearrange("p (m t) -> p t m", t=PACK),
+            )
+            for new, raw in ((wb, wb_raw), (wb_s, planes)):
+                heads = raw[:].rearrange("p (h c i) -> p h c i", h=H, c=2)
+                nc.vector.tensor_copy(
+                    out=new[:, 0, :].rearrange("p (h i) -> p h i", h=H), in_=heads[:, :, 0, :]
+                )
+                nc.vector.tensor_copy(
+                    out=new[:, 1, :].rearrange("p (e h i) -> p e h i", e=2, h=H),
+                    in_=heads[:, :, 1, :].rearrange("p h (i e) -> p e h i", e=2),
                 )
 
-        def rotate(g, j):
-            gj = g * J + j
-            qp = state["qp", g, j][:].rearrange("p b (h i e) -> p (b h) i e", h=H, e=2)
-            shape = [P, B * H, HALF, 2]
-            t1 = work.tile([P, B * H, HALF, 2], F32, bufs=4, name="t1")
-            t2 = work.tile([P, B * H, HALF, 2], F32, bufs=4, name="t2")
-            cos = trig[:, 0, gj, :].unsqueeze(1).unsqueeze(3).to_broadcast(shape)
-            sin = trig[:, 1:3, gj, :].rearrange("p e i -> p i e").unsqueeze(1).to_broadcast(shape)
-            nc.vector.tensor_tensor(out=t1[:], in0=qp, in1=cos, op=MULT)
-            nc.vector.tensor_tensor(out=t2[:], in0=qp[:, :, :, ::-1], in1=sin, op=MULT)
-            state["t", g, j] = (t1, t2)
-
-        def add_rotated(engine, g, j):
-            t1, t2 = state["t", g, j]
-            engine.tensor_tensor(
-                out=state["ot", g][:, :, j, ND:HD],
-                in0=t1[:].rearrange("p q i e -> p q (i e)"),
-                in1=t2[:].rearrange("p q i e -> p q (i e)"),
-                op=ADD,
-            )
-
-        def store(g):
-            nc.sync.dma_start(
-                out=out_view[g].rearrange("p q j d -> p q (j d)"),
-                in_=state["ot", g][:].rearrange("p q j d -> p q (j d)"),
-            )
+        STEPS = {
+            "K": widen_plain,
+            "B": widen,
+            "T": turn,
+            "D": quantise_x,
+            "A": project_latent,
+            "F": quantise_latent,
+            "S": project_sums,
+            "E": project_rotated,
+            "N": project_plain,
+            "M": rotate,
+            "R": add_and_store,
+            "f": turn_fractions,
+            "t": tables,
+            "W": arrange_weights,
+        }
 
         with tc.manual_schedule():
-            nc.vector.memset(planes[:].bitcast(I32), 0)
             nc.gpsimd.iota(
-                pos[:], pattern=[[P * J, GROUPS], [1, J]], base=0, channel_multiplier=J,
+                pos[:],
+                pattern=[[P * J, GROUPS], [1, J]],
+                base=0,
+                channel_multiplier=J,
                 allow_small_or_imprecise_dtypes=True,
             )
-            make_identity(nc, ident[:])
+            make_identity(nc, identity[:])
+
+            nc.sync.dma_start(
+                out=scale_row[:], in_=x_scale.rearrange("o q k -> (o q k)").partition_broadcast(P)
+            )
             load(0)
-            nc.scalar.dma_start(out=scale[:], in_=x_scale.rearrange("o q k -> (o q k)").partition_broadcast(P))
+            load(1)
+            nc.sync.dma_start(
+                out=scale_col[:], in_=x_scale.rearrange("o q (g p t) -> p (o q g) t", p=P, t=PACK)
+            )
             nc.sync.dma_start(
                 out=wa_raw[:], in_=wqa_words.rearrange("g p n t -> p g (n t)").bitcast(I32)
             )
-            for q in range(4):
+            nc.vector.memset(planes[:].bitcast(I32), 0)
+            for quadrant in range(4):
+                rows = slice(4 * quadrant, 4 * quadrant + 4)
                 nc.sync.dma_start(
-                    out=planes[32 * q : 32 * q + 8, :].bitcast(I32),
-                    in_=wqa_scales[:, 4 * q : 4 * q + 4, :].bitcast(I32),
+                    out=planes[32 * quadrant : 32 * quadrant + 8, :].bitcast(I32),
+                    in_=wqa_scales[:, rows, :].bitcast(I32),
                 )
-            for q in range(4):
+            for quadrant in range(4):
+                rows = slice(4 * quadrant, 4 * quadrant + 4)
                 nc.sync.dma_start(
-                    out=planes[32 * q + 8 : 32 * q + 12, :].bitcast(I32),
-                    in_=wqb_scales[0, 4 * q : 4 * q + 4, :].bitcast(I32),
+                    out=planes[32 * quadrant + 8 : 32 * quadrant + 12, :].bitcast(I32),
+                    in_=wqb_scales[0, rows, :].bitcast(I32),
                 )
+            nc.sync.dma_start(out=wb_raw[:], in_=wqb_words.rearrange("o p n t -> p (o n t)").bitcast(I32))
+            load(2)
+            load(3)
 
-            load(1)
-            wb_view = wqb_words.rearrange("o p (h c i) t -> c p (o h) (i t)", h=H, c=2)
-            for part in range(2):
-                nc.sync.dma_start(
-                    out=wb[:, part, :].rearrange("p (h i) -> p h i", h=H), in_=wb_view[part].bitcast(I32)
-                )
-
-            for i in range(HALF):
-                per_turn = 10000.0 ** (-2.0 * i / RD) / (2.0 * math.pi)
+            nc.vector.memset(freq[:, 0:1], 1.0)
+            nc.vector.tensor_scalar(
+                out=freq[:, 0:1], in0=freq[:, 0:1], scalar1=0.5 / math.pi, scalar2=None, op0=ALU.mult
+            )
+            n = 1
+            while n < HALF:
                 nc.vector.tensor_scalar(
-                    out=turns[:, :, i], in0=pos[:], scalar1=per_turn, scalar2=None, op0=MULT
+                    out=freq[:, n : 2 * n],
+                    in0=freq[:, 0:n],
+                    scalar1=10000.0 ** (-2.0 * n / RD),
+                    scalar2=None,
+                    op0=ALU.mult,
                 )
-            nc.vector.tensor_copy(out=whole_i[:], in_=turns[:])
-            nc.vector.tensor_copy(out=whole[:], in_=whole_i[:])
-            nc.vector.tensor_tensor(out=frac[:], in0=turns[:], in1=whole[:], op=SUB)
-            for n, shift in enumerate((0.0, 0.25, -0.25)):
-                nc.scalar.activation(
-                    out=fold[:, n, :], in_=frac[:].rearrange("p g i -> p (g i)"), func=AF.Abs, bias=shift
-                )
-            nc.scalar.activation(
-                out=fold2[:], in_=fold[:].rearrange("p n q -> p (n q)"), func=AF.Abs, bias=-0.5
-            )
-            nc.scalar.activation(
-                out=trig[:].rearrange("p n g i -> p (n g i)"), in_=fold2[:], func=AF.Sin,
-                bias=-0.5 * math.pi, scale=2.0 * math.pi,
+                n *= 2
+            nc.vector.tensor_tensor(
+                out=turns[:],
+                in0=pos[:].unsqueeze(2).to_broadcast([P, SLOTS, HALF]),
+                in1=freq[:].unsqueeze(1).to_broadcast([P, SLOTS, HALF]),
+                op=ALU.mult,
             )
 
-            for s in range(GROUPS + 4):
-                if s < GROUPS:
-                    xs = work.tile([P, TILES, D], BF16, align_bytes=64, name="xs")
-                    xg = mid.tile([P, 2, TOK * 4], BF16, align_bytes=64, name="xg")
-                    state["xs", s], state["xg", s] = xs, xg
-                    if s + 2 < GROUPS:
-                        load(s + 2)
-                if s in SCALAR_GROUPS:
-                    for tile in range(2):
-                        cast(s, tile, 512, D)
-                if s == 2:
-                    nc.vector.tensor_copy(
-                        out=wa[:].rearrange("p g (t m) -> p g t m", t=4),
-                        in_=wa_raw[:].rearrange("p g (m t) -> p g t m", t=4),
-                    )
-                    nc.vector.tensor_copy(
-                        out=wa_s[:].rearrange("p (t m) -> p t m", t=4),
-                        in_=planes[:].rearrange("p (m t) -> p t m", t=4),
-                    )
-                    nc.vector.tensor_copy(
-                        out=wb_s[:].rearrange("p c (h i) -> p c h i", h=H),
-                        in_=planes[:].rearrange("p (h c i) -> p c h i", h=H, c=2),
-                    )
-                if 0 <= s - 2 < GROUPS:
-                    quant_x(s - 2)
-                    project_a(s - 2)
-                if 0 <= s - 4:
-                    rotate(s - 4, 0)
-                    rotate(s - 4, 1)
-                if 0 <= s - 3 < GROUPS:
-                    ot = outs.tile([P, B * H, J, HD], F32, name="ot")
-                    state["ot", s - 3] = ot
-                    quant_q(s - 3)
-                    for part in (1, 0):
-                        for j in range(J):
-                            project_b(s - 3, part, j)
-                if 0 <= s - 4:
-                    add_rotated(nc.vector, s - 4, 0)
-                    add_rotated(nc.vector, s - 4, 1)
-                    store(s - 4)
-                if s < GROUPS:
-                    for pair in range(2):
-                        on_scalar = s in SCALAR_GROUPS and pair == 0
-                        for tile in (2 * pair, 2 * pair + 1):
-                            widen(s, tile, 0, 512 if on_scalar else D)
-                        if on_scalar:
-                            turn(s, pair, 1, False)
-                            turn(s, pair, 0, True)
-                        else:
-                            turn(s, pair, 0, True)
-                            turn(s, pair, 1, True)
+            for word in ORDER.split():
+                STEPS[word[0]](*[int(digit) for digit in word[1:]])

@@ -31,14 +31,15 @@ FP8X4 = mybir.dt.float8_e4m3fn_x4
 ALU = mybir.AluOpType
 AF = mybir.ActivationFunctionType
 
-SCALAR_GROUPS = (1, 3, 4, 6)
+SCALAR_GROUPS = (4, 6)
+FIRST = (0, 0)
 
 ORDER = """
-f K1 B00 B01 t0 B02 B03 T00 W B10 t1 B11 T01 t2 B12 T10 D0 A00 B13 B20 B21 T11 B22 A01 K3 D1 T20 B23 A10 B30 B31
-T21 F0 B32 A11 T30 S0 E00 N00 E01 B33 D2 B40 T31 F1 B41 B42 B43 M0 B50 B51 N01 B52 K4 D3 R0 A20 N10 A21 T40 S1
-A30 E10 F2 E11 T41 N11 M1 A31 N20 B53 B60 K6 B61 D4 T50 B62 E20 A40 N21 T51 B63 E21 F3 B70 S2 N30 R1 A41 T60 M2
-N31 E30 E31 D5 S3 F4 B71 M3 B72 A50 T61 E40 N40 R2 D6 A51 T70 S4 N41 E41 B73 A60 T71 F5 M4 R3 N50 A61 E50 N51
-E51 S5 D7 A70 R4 F6 M5 N60 S6 E60 E61 M6 R5 A71 N61 F7 S7 E70 R6 N70 E71 M7 N71 R7
+f C00 L T00 B02 B03 B10 B11 T01 B12 t0 T10 B13 W D0 A00 T11 B20 B21 B22 A01 B23 B30 B31 t1 F0 D1 T20 B32 K4 B33
+B40 B41 S0 T21 t2 A10 D2 B42 E00 N00 T30 E01 B43 B50 A11 B51 M0 T31 A20 N01 A21 F1 B52 N10 T40 N11 D3 A30 B53 F2
+E10 R0 B60 B61 E11 S1 B62 M1 T50 N20 A31 T41 K6 N21 B63 B70 E20 D4 E21 T51 S2 A40 F3 T60 M2 A41 E30 E31 D5 R1
+B71 S3 M3 F4 R2 N30 T61 A50 E40 E41 D6 B72 T70 A51 N31 S4 B73 A60 R3 N40 T71 A61 F5 M4 N41 E50 D7 S5 A70 E51 N50
+R4 A71 M5 N51 F6 R5 S6 E60 E61 N60 N61 M6 F7 S7 N70 E70 R6 E71 M7 N71 R7
 """
 
 
@@ -49,7 +50,8 @@ def tile_mlaattention_pa_t_w8_kernel(
     with ExitStack() as ctx:
         keep = ctx.enter_context(tc.tile_pool(name="keep", bufs=1))
         xin = ctx.enter_context(tc.tile_pool(name="xin", bufs=4))
-        turned = ctx.enter_context(tc.tile_pool(name="turned", bufs=3))
+        wide = ctx.enter_context(tc.tile_pool(name="wide", bufs=3))
+        turned = ctx.enter_context(tc.tile_pool(name="turned", bufs=4))
         work = ctx.enter_context(tc.tile_pool(name="work", bufs=2))
         outs = ctx.enter_context(tc.tile_pool(name="outs", bufs=4))
         ps_turn = ctx.enter_context(tc.psum_pool(name="ps_turn", bufs=2))
@@ -62,6 +64,7 @@ def tile_mlaattention_pa_t_w8_kernel(
         out_view = out.rearrange("b h (g p j) d -> g p (b h) (j d)", p=P, j=J)
 
         identity = keep.tile([P, P], F32, name="identity")
+        scale_eight = keep.tile([P, D // P], F32, name="scale_eight")
         scale_row = keep.tile([P, D], F32, name="scale_row")
         scale_col = keep.tile([P, KP, PACK], F32, name="scale_col")
         wa_raw = keep.tile([P, KP, QL], I32, align_bytes=64, name="wa_raw")
@@ -89,11 +92,13 @@ def tile_mlaattention_pa_t_w8_kernel(
 
         def open_group(g):
             if ("wide", g) not in held:
-                held["wide", g] = work.tile([P, TILES, D], BF16, align_bytes=64, name="wide")
+                held["wide", g] = wide.tile([P, TILES, D], BF16, align_bytes=64, name="wide_x")
                 held["turned", g] = turned.tile([P, KP, TOK * PACK], BF16, align_bytes=64, name="turned_x")
 
-        def split(g, tile):
-            return KP - 1 if g in SCALAR_GROUPS and tile < J else KP
+        def split(g, b):
+            if (g, b) == FIRST:
+                return 0
+            return KP - 1 if g in SCALAR_GROUPS and b == 0 else KP
 
         def fp8_view(g, tile, k0, k1):
             b, j = divmod(tile, J)
@@ -101,13 +106,28 @@ def tile_mlaattention_pa_t_w8_kernel(
 
         def widen_plain(g):
             open_group(g)
+            k0 = split(g, 0) * K_PASS
             for tile in range(J):
-                k0 = split(g, tile) * K_PASS
                 nc.scalar.copy(out=held["wide", g][:, tile, k0:D], in_=fp8_view(g, tile, k0, D))
+
+        def widen_first(g, b):
+            open_group(g)
+            nc.vector.tensor_copy(
+                out=held["wide", g][:, b * J : (b + 1) * J, :].rearrange("p j k -> p (j k)"),
+                in_=held["bytes", g][:, b, :].bitcast(FP8),
+            )
+
+        def spread_scales():
+            by_eight = scale_row[:].rearrange("p (n m) -> p n m", n=P)
+            for half in range(2):
+                nc.scalar.copy(
+                    out=by_eight[:, :, half * PACK : (half + 1) * PACK],
+                    in_=held["scales", half][:].rearrange("p c n -> p n c"),
+                )
 
         def widen(g, tile):
             open_group(g)
-            k1 = split(g, tile) * K_PASS
+            k1 = split(g, tile // J) * K_PASS
             nc.vector.tensor_tensor(
                 out=held["wide", g][:, tile, 0:k1], in0=fp8_view(g, tile, 0, k1), in1=scale_row[:, 0:k1], op=ALU.mult
             )
@@ -115,14 +135,14 @@ def tile_mlaattention_pa_t_w8_kernel(
                 load(g + 4)
 
         def turn(g, b):
-            for kp in range(KP - 1, -1, -1) if split(g, b * J) < KP else range(KP):
+            for kp in reversed(range(KP)) if split(g, b) == KP - 1 else range(KP):
                 bank = ps_turn.tile([P, J, 2, P], F32, name="bank_t")
                 for j in range(J):
                     words = held["wide", g][:, b * J + j, kp * K_PASS : (kp + 1) * K_PASS].bitcast(F32)
                     for u in range(2):
                         nc.tensor.transpose(bank[:, j, u, :], words[:, u::2], identity[:])
                 dst = held["turned", g][:, kp, b * PAIR * PACK : (b + 1) * PAIR * PACK]
-                if kp < split(g, b * J):
+                if kp < split(g, b):
                     nc.scalar.copy(
                         out=dst.bitcast(F32).rearrange("p (j r u) -> p j r u", j=J, u=2),
                         in_=bank[:].rearrange("p j u r -> p j r u"),
@@ -295,6 +315,8 @@ def tile_mlaattention_pa_t_w8_kernel(
                 )
 
         STEPS = {
+            "C": widen_first,
+            "L": spread_scales,
             "K": widen_plain,
             "B": widen,
             "T": turn,
@@ -321,17 +343,16 @@ def tile_mlaattention_pa_t_w8_kernel(
             )
             make_identity(nc, identity[:])
 
-            nc.sync.dma_start(
-                out=scale_row[:], in_=x_scale.rearrange("o q k -> (o q k)").partition_broadcast(P)
-            )
+            nc.scalar.dma_start(out=scale_eight[:], in_=x_scale.rearrange("o q (n m) -> n (o q m)", n=P))
             load(0)
-            load(1)
-            nc.sync.dma_start(
+            nc.scalar.dma_start(
                 out=scale_col[:], in_=x_scale.rearrange("o q (g p t) -> p (o q g) t", p=P, t=PACK)
             )
+            load(1)
             nc.sync.dma_start(
                 out=wa_raw[:], in_=wqa_words.rearrange("g p n t -> p g (n t)").bitcast(I32)
             )
+            nc.sync.dma_start(out=wb_raw[:], in_=wqb_words.rearrange("o p n t -> p (o n t)").bitcast(I32))
             nc.vector.memset(planes[:].bitcast(I32), 0)
             for quadrant in range(4):
                 rows = slice(4 * quadrant, 4 * quadrant + 4)
@@ -345,7 +366,6 @@ def tile_mlaattention_pa_t_w8_kernel(
                     out=planes[32 * quadrant + 8 : 32 * quadrant + 12, :].bitcast(I32),
                     in_=wqb_scales[0, rows, :].bitcast(I32),
                 )
-            nc.sync.dma_start(out=wb_raw[:], in_=wqb_words.rearrange("o p n t -> p (o n t)").bitcast(I32))
             load(2)
             load(3)
 
@@ -369,6 +389,15 @@ def tile_mlaattention_pa_t_w8_kernel(
                 in1=freq[:].unsqueeze(1).to_broadcast([P, SLOTS, HALF]),
                 op=ALU.mult,
             )
+
+            for half in range(2):
+                bank = ps_latent.tile([P, PACK, P], F32, name="bank_l")
+                held["scales", half] = bank
+                for c in range(PACK):
+                    m = half * PACK + c
+                    nc.tensor.transpose(
+                        bank[:, c, :], scale_eight[:, m : m + 1].to_broadcast([P, P]), identity[:]
+                    )
 
             for word in ORDER.split():
                 STEPS[word[0]](*[int(digit) for digit in word[1:]])

import math
from contextlib import ExitStack

import concourse.mybir as mybir
from concourse.masks import make_identity

B, S, D, QL = 2, 2048, 1024, 512
H, ND, RD = 4, 64, 64
HD = ND + RD
HALF = RD // 2
P = 128
J = 2
TILES = B * J
TOK = TILES * P
GROUPS = B * S // TOK
PAIR = 2 * P
PACK = 4
KP = D // (P * PACK)
K_PASS = P * PACK
PAIRS = H * HALF
SLOTS = GROUPS * J
LAST_STORES = 4
FLOPS = 2 * B * S * QL * (D + H * HD)

F32 = mybir.dt.float32
BF16 = mybir.dt.bfloat16
I32 = mybir.dt.int32
U8 = mybir.dt.uint8
FP8 = mybir.dt.float8_e4m3fn
FP8X4 = mybir.dt.float8_e4m3fn_x4
ALU = mybir.AluOpType
AF = mybir.ActivationFunctionType

SCALAR_GROUPS = (4, 6)
FIRST = (0, 0)

ORDER = """
f C00 L T00 B02 B03 B10 B11 T01 B12 t0 T10 B13 W D0 A00 T11 B20 B21 B22 A01 B23 B30 B31 t1 F0 D1 T20 B32 K4 B33
B40 B41 S0 T21 t2 A10 D2 B42 E00 N00 T30 E01 B43 B50 A11 B51 M0 T31 A20 N01 A21 F1 B52 N10 T40 N11 D3 A30 B53 F2
E10 R0 B60 B61 E11 S1 B62 M1 T50 N20 A31 T41 K6 N21 B63 B70 E20 D4 E21 T51 S2 A40 F3 T60 M2 A41 E30 E31 D5 R1
B71 S3 M3 F4 R2 N30 T61 A50 E40 E41 D6 B72 T70 A51 N31 S4 B73 A60 R3 N40 T71 A61 F5 M4 N41 E50 D7 S5 A70 E51 N50
R4 A71 M5 N51 F6 R5 S6 E60 E61 N60 N61 M6 F7 S7 N70 E70 R6 E71 M7 N71 R7
"""


def tile_mlaattention_pa_t_w8_kernel(
    tc, x_bytes, x_scale, wqa_words, wqa_scales, wqb_words, wqb_scales, out
):
    nc = tc.nc
    with ExitStack() as ctx:
        keep = ctx.enter_context(tc.tile_pool(name="keep", bufs=1))
        xin = ctx.enter_context(tc.tile_pool(name="xin", bufs=4))
        wide = ctx.enter_context(tc.tile_pool(name="wide", bufs=3))
        turned = ctx.enter_context(tc.tile_pool(name="turned", bufs=4))
        work = ctx.enter_context(tc.tile_pool(name="work", bufs=2))
        outs = ctx.enter_context(tc.tile_pool(name="outs", bufs=4))
        ps_turn = ctx.enter_context(tc.psum_pool(name="ps_turn", bufs=2))
        ps_latent = ctx.enter_context(tc.psum_pool(name="ps_latent", bufs=2))
        ps_rot = ctx.enter_context(tc.psum_pool(name="ps_rot", bufs=2))
        ps_sum = ctx.enter_context(tc.psum_pool(name="ps_sum", bufs=1))
        ps_plain = ctx.enter_context(tc.psum_pool(name="ps_plain", bufs=1))

        x_view = x_bytes.rearrange("b (g p j) k -> g p b (j k)", p=P, j=J)
        out_view = out.rearrange("b h (g p j) d -> g p (b h) (j d)", p=P, j=J)

        identity = keep.tile([P, P], F32, name="identity")
        scale_eight = keep.tile([P, D // P], F32, name="scale_eight")
        scale_row = keep.tile([P, D], F32, name="scale_row")
        scale_col = keep.tile([P, KP, PACK], F32, name="scale_col")
        wa_raw = keep.tile([P, KP, QL], I32, align_bytes=64, name="wa_raw")
        wa = keep.tile([P, KP, QL], I32, align_bytes=64, name="wa")
        wb_raw = keep.tile([P, H * HD], I32, align_bytes=64, name="wb_raw")
        wb = keep.tile([P, 2, H * ND], I32, align_bytes=64, name="wb")
        planes = keep.tile([P, QL], U8, align_bytes=64, name="planes")
        wa_s = keep.tile([P, QL], U8, align_bytes=64, name="wa_s")
        wb_s = keep.tile([P, 2, H * ND], U8, align_bytes=64, name="wb_s")
        pos = keep.tile([P, SLOTS], F32, name="pos")
        freq = keep.tile([P, HALF], F32, name="freq")
        turns = keep.tile([P, SLOTS, HALF], F32, name="turns")
        whole_i = keep.tile([P, SLOTS, HALF], I32, name="whole_i")
        whole = keep.tile([P, SLOTS, HALF], F32, name="whole")
        frac = keep.tile([P, SLOTS, HALF], F32, name="frac")
        fold = keep.tile([P, 3, SLOTS, HALF], F32, name="fold")
        trig = keep.tile([P, 3, SLOTS, HALF], F32, name="trig")
        cross = keep.tile([P, 2, SLOTS, HALF], F32, name="cross")

        held = {}

        def load(g):
            held["bytes", g] = xin.tile([P, B, J * D], U8, name="x_tile")
            nc.sync.dma_start(out=held["bytes", g][:], in_=x_view[g])

        def open_group(g):
            if ("wide", g) not in held:
                held["wide", g] = wide.tile([P, TILES, D], BF16, align_bytes=64, name="wide_x")
                held["turned", g] = turned.tile([P, KP, TOK * PACK], BF16, align_bytes=64, name="turned_x")

        def split(g, b):
            if (g, b) == FIRST:
                return 0
            return KP - 1 if g in SCALAR_GROUPS and b == 0 else KP

        def fp8_view(g, tile, k0, k1):
            b, j = divmod(tile, J)
            return held["bytes", g][:, b, j * D + k0 : j * D + k1].bitcast(FP8)

        def widen_plain(g):
            open_group(g)
            k0 = split(g, 0) * K_PASS
            for tile in range(J):
                nc.scalar.copy(out=held["wide", g][:, tile, k0:D], in_=fp8_view(g, tile, k0, D))

        def widen_first(g, b):
            open_group(g)
            nc.vector.tensor_copy(
                out=held["wide", g][:, b * J : (b + 1) * J, :].rearrange("p j k -> p (j k)"),
                in_=held["bytes", g][:, b, :].bitcast(FP8),
            )

        def spread_scales():
            by_eight = scale_row[:].rearrange("p (n m) -> p n m", n=P)
            for half in range(2):
                nc.scalar.copy(
                    out=by_eight[:, :, half * PACK : (half + 1) * PACK],
                    in_=held["scales", half][:].rearrange("p c n -> p n c"),
                )

        def widen(g, tile):
            open_group(g)
            k1 = split(g, tile // J) * K_PASS
            nc.vector.tensor_tensor(
                out=held["wide", g][:, tile, 0:k1], in0=fp8_view(g, tile, 0, k1), in1=scale_row[:, 0:k1], op=ALU.mult
            )
            if tile == TILES - 1 and g + 4 < GROUPS:
                load(g + 4)

        def turn(g, b):
            for kp in reversed(range(KP)) if split(g, b) == KP - 1 else range(KP):
                bank = ps_turn.tile([P, J, 2, P], F32, name="bank_t")
                for j in range(J):
                    words = held["wide", g][:, b * J + j, kp * K_PASS : (kp + 1) * K_PASS].bitcast(F32)
                    for u in range(2):
                        nc.tensor.transpose(bank[:, j, u, :], words[:, u::2], identity[:])
                dst = held["turned", g][:, kp, b * PAIR * PACK : (b + 1) * PAIR * PACK]
                if kp < split(g, b):
                    nc.scalar.copy(
                        out=dst.bitcast(F32).rearrange("p (j r u) -> p j r u", j=J, u=2),
                        in_=bank[:].rearrange("p j u r -> p j r u"),
                    )
                else:
                    planar = work.tile([P, PACK, PAIR], BF16, name="planar")
                    values = bank[:].rearrange("p j u r -> p (j u r)").bitcast(BF16)
                    values = values.rearrange("p (j u r e) -> p j u r e", j=J, u=2, e=2)
                    for t in range(PACK):
                        u, e = divmod(t, 2)
                        nc.scalar.activation(
                            out=planar[:, t, :].rearrange("p (j r) -> p j r", j=J),
                            in_=values[:, :, u, :, e],
                            func=AF.Copy,
                            scale=scale_col[:, kp, t : t + 1],
                        )
                    nc.scalar.copy(
                        out=dst.rearrange("p (n t) -> p n t", t=PACK), in_=planar[:].rearrange("p t n -> p n t")
                    )

        def quantise_x(g):
            held["xq", g] = work.tile([P, KP, TOK], I32, align_bytes=64, name="xq")
            held["xq_s", g] = work.tile([P, KP, TOK], U8, align_bytes=64, name="xq_s")
            for kp in range(KP):
                nc.vector.quantize_mx(
                    out=held["xq", g][:, kp, :].bitcast(FP8X4),
                    scales=held["xq_s", g][:, kp, :],
                    in_=held["turned", g][:, kp, :],
                )

        def project_latent(g, half):
            if half == 0:
                held["latent", g] = work.tile([P, TOK * PACK], BF16, align_bytes=64, name="latent")
            for tile in range(half * J, (half + 1) * J):
                tokens = slice(tile * P, (tile + 1) * P)
                bank = ps_latent.tile([P, PACK, P], F32, name="bank_l")
                for t in range(PACK):
                    channels = slice(t * P, (t + 1) * P)
                    for kp in range(KP):
                        nc.tensor.matmul_mx(
                            out=bank[:, t, :],
                            lhsT=wa[:, kp, channels].bitcast(FP8X4),
                            lhsT_scale=wa_s[4 * kp :, channels],
                            rhs=held["xq", g][:, kp, tokens].bitcast(FP8X4),
                            rhs_scale=held["xq_s", g][:, kp, tokens],
                            start=(kp == 0),
                            stop=(kp == KP - 1),
                        )
                nc.scalar.copy(
                    out=held["latent", g][:, tile * P * PACK : (tile + 1) * P * PACK].rearrange(
                        "p (n t) -> p n t", t=PACK
                    ),
                    in_=bank[:].rearrange("p t n -> p n t"),
                )

        def quantise_latent(g):
            held["lq", g] = work.tile([P, TOK], I32, align_bytes=64, name="lq")
            held["lq_s", g] = work.tile([P, TOK], U8, align_bytes=64, name="lq_s")
            nc.vector.quantize_mx(
                out=held["lq", g][:].bitcast(FP8X4), scales=held["lq_s", g][:], in_=held["latent", g][:]
            )

        def project_q(g, tile, part, c0, c1, bank, start, stop):
            tokens = slice(tile * P, (tile + 1) * P)
            nc.tensor.matmul_mx(
                out=bank,
                lhsT=held["lq", g][:, tokens].bitcast(FP8X4),
                lhsT_scale=held["lq_s", g][:, tokens],
                rhs=wb[:, part, c0:c1].bitcast(FP8X4),
                rhs_scale=wb_s[8:, part, c0:c1],
                start=start,
                stop=stop,
            )

        def project_sums(g):
            bank = ps_sum.tile([P, J, B, PAIRS], F32, name="bank_s")
            held["sums", g] = bank
            for j in range(J):
                for b in range(B):
                    for e in range(2):
                        project_q(
                            g, b * J + j, 1, e * PAIRS, (e + 1) * PAIRS, bank[:, j, b, :], e == 0, e == 1
                        )

        def project_rotated(g, j):
            bank = ps_rot.tile([P, 2, B, PAIRS], F32, name="bank_r")
            held["rot", g, j] = bank
            for b in range(B):
                for e in range(2):
                    project_q(g, b * J + j, 1, e * PAIRS, (e + 1) * PAIRS, bank[:, e, b, :], True, True)

        def project_plain(g, j):
            if j == 0:
                held["out", g] = outs.tile([P, B * H, J, HD], F32, name="out_tile")
            bank = ps_plain.tile([P, B, H * ND], F32, name="bank_p")
            for b in range(B):
                project_q(g, b * J + j, 0, 0, H * ND, bank[:, b, :], True, True)
            nc.scalar.copy(
                out=held["out", g][:, :, j, 0:ND], in_=bank[:].rearrange("p b (h d) -> p (b h) d", d=ND)
            )

        def rotate(g):
            shared = work.tile([P, J, B * H, HALF], F32, name="shared")
            other = work.tile([P, J, B * H, HALF, 2], F32, name="other")
            held["products", g] = (shared, other)
            nc.vector.tensor_tensor(
                out=shared[:],
                in0=held["sums", g][:].rearrange("p j b (h i) -> p j (b h) i", h=H),
                in1=trig[:, 0, g * J : (g + 1) * J, :].unsqueeze(2).to_broadcast([P, J, B * H, HALF]),
                op=ALU.mult,
            )
            for j in range(J):
                pairs = held["rot", g, j][:].rearrange("p e b (h i) -> p (b h) i e", h=H)
                factors = cross[:, :, g * J + j, :].rearrange("p e i -> p i e").unsqueeze(1)
                nc.vector.tensor_tensor(
                    out=other[:, j],
                    in0=pairs[:, :, :, ::-1],
                    in1=factors.to_broadcast([P, B * H, HALF, 2]),
                    op=ALU.mult,
                )

        def add_and_store(g):
            shared, other = held["products", g]
            size = B * H // (LAST_STORES if g == GROUPS - 1 else 1)
            for q0 in range(0, B * H, size):
                q = slice(q0, q0 + size)
                nc.vector.tensor_tensor(
                    out=held["out", g][:, q, :, ND:HD].rearrange("p q j (i e) -> p j q i e", e=2),
                    in0=shared[:, :, q, :].unsqueeze(4).to_broadcast([P, J, size, HALF, 2]),
                    in1=other[:, :, q],
                    op=ALU.add,
                )
                nc.sync.dma_start(
                    out=out_view[g][:, q], in_=held["out", g][:, q].rearrange("p q j d -> p q (j d)")
                )

        def turn_fractions():
            nc.vector.tensor_copy(out=whole_i[:], in_=turns[:])
            nc.vector.tensor_copy(out=whole[:], in_=whole_i[:])
            nc.vector.tensor_tensor(out=frac[:], in0=turns[:], in1=whole[:], op=ALU.subtract)

        def tables(part):
            if part == 0:
                for n, shift in enumerate((0.0, -0.125, 0.125)):
                    nc.scalar.activation(out=fold[:, n], in_=frac[:], func=AF.Abs, bias=shift)
            elif part == 1:
                nc.scalar.activation(
                    out=trig[:], in_=fold[:], func=AF.Sin, bias=0.5 * math.pi, scale=-2.0 * math.pi
                )
            else:
                nc.scalar.mul(out=cross[:], in_=trig[:, 1:3], mul=-math.sqrt(2.0))

        def arrange_weights():
            nc.vector.tensor_copy(
                out=wa[:].rearrange("p g (t m) -> p g t m", t=PACK),
                in_=wa_raw[:].rearrange("p g (m t) -> p g t m", t=PACK),
            )
            nc.vector.tensor_copy(
                out=wa_s[:].rearrange("p (t m) -> p t m", t=PACK),
                in_=planes[:].rearrange("p (m t) -> p t m", t=PACK),
            )
            for new, raw in ((wb, wb_raw), (wb_s, planes)):
                heads = raw[:].rearrange("p (h c i) -> p h c i", h=H, c=2)
                nc.vector.tensor_copy(
                    out=new[:, 0, :].rearrange("p (h i) -> p h i", h=H), in_=heads[:, :, 0, :]
                )
                nc.vector.tensor_copy(
                    out=new[:, 1, :].rearrange("p (e h i) -> p e h i", e=2, h=H),
                    in_=heads[:, :, 1, :].rearrange("p h (i e) -> p e h i", e=2),
                )

        STEPS = {
            "C": widen_first,
            "L": spread_scales,
            "K": widen_plain,
            "B": widen,
            "T": turn,
            "D": quantise_x,
            "A": project_latent,
            "F": quantise_latent,
            "S": project_sums,
            "E": project_rotated,
            "N": project_plain,
            "M": rotate,
            "R": add_and_store,
            "f": turn_fractions,
            "t": tables,
            "W": arrange_weights,
        }

        with tc.manual_schedule():
            nc.gpsimd.iota(
                pos[:],
                pattern=[[P * J, GROUPS], [1, J]],
                base=0,
                channel_multiplier=J,
                allow_small_or_imprecise_dtypes=True,
            )
            make_identity(nc, identity[:])

            nc.scalar.dma_start(out=scale_eight[:], in_=x_scale.rearrange("o q (n m) -> n (o q m)", n=P))
            load(0)
            nc.scalar.dma_start(
                out=scale_col[:], in_=x_scale.rearrange("o q (g p t) -> p (o q g) t", p=P, t=PACK)
            )
            load(1)
            nc.sync.dma_start(
                out=wa_raw[:], in_=wqa_words.rearrange("g p n t -> p g (n t)").bitcast(I32)
            )
            nc.sync.dma_start(out=wb_raw[:], in_=wqb_words.rearrange("o p n t -> p (o n t)").bitcast(I32))
            nc.vector.memset(planes[:].bitcast(I32), 0)
            for quadrant in range(4):
                rows = slice(4 * quadrant, 4 * quadrant + 4)
                nc.sync.dma_start(
                    out=planes[32 * quadrant : 32 * quadrant + 8, :].bitcast(I32),
                    in_=wqa_scales[:, rows, :].bitcast(I32),
                )
            for quadrant in range(4):
                rows = slice(4 * quadrant, 4 * quadrant + 4)
                nc.sync.dma_start(
                    out=planes[32 * quadrant + 8 : 32 * quadrant + 12, :].bitcast(I32),
                    in_=wqb_scales[0, rows, :].bitcast(I32),
                )
            load(2)
            load(3)

            nc.vector.memset(freq[:, 0:1], 1.0)
            nc.vector.tensor_scalar(
                out=freq[:, 0:1], in0=freq[:, 0:1], scalar1=0.5 / math.pi, scalar2=None, op0=ALU.mult
            )
            n = 1
            while n < HALF:
                nc.vector.tensor_scalar(
                    out=freq[:, n : 2 * n],
                    in0=freq[:, 0:n],
                    scalar1=10000.0 ** (-2.0 * n / RD),
                    scalar2=None,
                    op0=ALU.mult,
                )
                n *= 2
            nc.vector.tensor_tensor(
                out=turns[:],
                in0=pos[:].unsqueeze(2).to_broadcast([P, SLOTS, HALF]),
                in1=freq[:].unsqueeze(1).to_broadcast([P, SLOTS, HALF]),
                op=ALU.mult,
            )

            for half in range(2):
                bank = ps_latent.tile([P, PACK, P], F32, name="bank_l")
                held["scales", half] = bank
                for c in range(PACK):
                    m = half * PACK + c
                    nc.tensor.transpose(
                        bank[:, c, :], scale_eight[:, m : m + 1].to_broadcast([P, P]), identity[:]
                    )

            for word in ORDER.split():
                STEPS[word[0]](*[int(digit) for digit in word[1:]])
